import numpy as np
import ml_dtypes


def mxq(x, axis, fmt="e4m3"):
    dtype, down = {"e4m3": (ml_dtypes.float8_e4m3fn, 7), "e5m2": (ml_dtypes.float8_e5m2, 14)}[fmt]
    v = np.moveaxis(np.asarray(x, np.float32).astype(ml_dtypes.bfloat16).astype(np.float64), axis, -1)
    blocks = v.reshape(v.shape[:-1] + (-1, 32))
    amax = np.abs(blocks).max(-1, keepdims=True)
    byte = np.maximum(np.where(amax > 0, np.frexp(amax)[1] - 1 + 127, 0) - down, 1)
    scale = np.exp2(byte - 127.0)
    codes = (blocks / scale).astype(np.float32).astype(dtype).astype(np.float64)
    return np.moveaxis((codes * scale).reshape(v.shape), -1, axis)


WIDE = False


def mx_kscale(k):
    if not WIDE:
        return np.ones(k)
    levels = np.array([10, -10, 5, -5, 0])
    a = np.random.permutation(np.resize(levels, k // 512 * 4)).reshape(k // 512, 4)
    idx = np.arange(k)
    return np.exp2(a[idx // 512, idx % 128 // 32])


BF16 = ml_dtypes.bfloat16


def bf(x):
    return np.asarray(x, np.float32).astype(BF16)


def f64(x):
    return np.asarray(x).astype(np.float64)


S, HID, NH, Q_LORA, KV_LORA, NOPE, ROPE, VDIM, BLK = 8192, 512, 4, 512, 512, 64, 64, 128, 128
HEAD = NOPE + ROPE
EPS = 1e-6


def blockscale(rows, cols, k, g):
    return bf((np.random.random((rows, cols)) * 0.8 + 0.2) * g / np.sqrt(k))


def dequant(w, s):
    so = np.repeat(s, BLK, axis=0)[: w.shape[0]]
    se = np.repeat(so, BLK, axis=1)[:, : w.shape[1]]
    return w * se


def rmsnorm(x, w):
    var = np.mean(x * x, axis=-1, keepdims=True)
    return x * (1.0 / np.sqrt(var + EPS)) * w


def rotate_half(x):
    h = x.shape[-1] // 2
    return np.concatenate([-x[..., h:], x[..., :h]], axis=-1)


def setup_inputs():
    s, t = mx_kscale(HID), mx_kscale(Q_LORA)
    ang = np.arange(S)[:, None] / (10000.0 ** (np.arange(0, ROPE, 2) / ROPE))[None, :]
    ang = np.concatenate([ang, ang], axis=-1)
    return {"hidden_states": bf(np.random.standard_normal((S, HID)) * s),
            "cos": bf(np.cos(ang)),
            "sin": bf(np.sin(ang)),
            "wq_a": bf(np.random.standard_normal((Q_LORA, HID)) / s[None, :]),
            "sq_a": blockscale(Q_LORA // BLK, HID // BLK, HID, 1.0),
            "wq_b": bf(np.random.standard_normal((NH * HEAD, Q_LORA)) / t[None, :]),
            "sq_b": blockscale(NH * HEAD // BLK, Q_LORA // BLK, Q_LORA, 2.0),
            "q_ln_w": bf((1.0 + 0.1 * np.random.standard_normal(Q_LORA)) * t)}


def reference(hidden_states, cos, sin, wq_a, sq_a, wq_b, sq_b, q_ln_w):
    wa = dequant(f64(wq_a), f64(sq_a))
    lq = mxq(f64(hidden_states), 1, "e4m3") @ mxq(wa, 1, "e4m3").T
    h = rmsnorm(lq, f64(q_ln_w))
    wb = dequant(f64(wq_b), f64(sq_b))
    q = (mxq(h, 1, "e4m3") @ mxq(wb, 1, "e4m3").T).reshape(S, NH, HEAD)
    q_nope, q_pe = q[..., :NOPE], q[..., NOPE:]
    q_rot = q_pe * f64(cos)[:, None, :] + rotate_half(q_pe) * f64(sin)[:, None, :]
    return q_nope, q_rot

@@ -1,0 +1,303 @@
+from contextlib import ExitStack
+
+import concourse.mybir as mybir
+from concourse.masks import make_identity
+
+BF16 = mybir.dt.bfloat16
+F32 = mybir.dt.float32
+U32 = mybir.dt.uint32
+U8 = mybir.dt.uint8
+FP8X4 = mybir.dt.float8_e4m3fn_x4
+ACT = mybir.ActivationFunctionType
+ALU = mybir.AluOpType
+
+P = 128
+PACK = 4
+K = P * PACK
+HALVES = 2
+TOKENS = 8192
+TILES = TOKENS // P
+UNIT_TILES = 2
+UNITS = TILES // UNIT_TILES
+LOAD_TILES = 4
+X_LOADS = TILES // LOAD_TILES
+TABLE_TILES = 16
+HEADS = 4
+NOPE = 64
+ROPE = 64
+HALF = ROPE // 2
+OUT = HEADS * (NOPE + ROPE)
+ROW_TILES = OUT // P
+BLOCKS = K // P
+EPS = 1e-6
+X_LEAD = 2
+Q_LAG = 3
+WB_TRANSPOSE_ROUND = 1
+WB_QUANTISE_ROUND = 2
+
+FLOPS = 2 * 2 * TOKENS * K * OUT
+
+
+def tile_deepseekv3attention_pa_t_kernel(
+    tc, hidden_states, cos, sin, wq_a, sq_a, wq_b, sq_b, q_ln_w, out_0, out_1
+):
+    nc = tc.nc
+    x_dram = hidden_states.rearrange("(p t) k -> p t k", t=TILES)
+    cos_dram = cos.rearrange("(p t) d -> p t d", t=TILES)
+    sin_dram = sin.rearrange("(p t) d -> p t d", t=TILES)
+    nope_dram = out_0.rearrange("(p t) h d -> p t (h d)", t=TILES)
+    rot_dram = out_1.rearrange("(p t) h d -> p t (h d)", t=TILES)
+
+    with ExitStack() as ctx:
+        keep = ctx.enter_context(tc.tile_pool(name="keep", bufs=1))
+        x_pool = ctx.enter_context(tc.tile_pool(name="x", bufs=X_LOADS))
+        work = ctx.enter_context(tc.tile_pool(name="work", bufs=3))
+        results = ctx.enter_context(tc.tile_pool(name="results", bufs=4))
+        psum_words = ctx.enter_context(tc.psum_pool(name="psum_words", bufs=1))
+        psum_lq = ctx.enter_context(tc.psum_pool(name="psum_lq", bufs=2 * UNIT_TILES))
+        psum_q = ctx.enter_context(tc.psum_pool(name="psum_q", bufs=1))
+        ctx.enter_context(tc.manual_schedule())
+
+        sa_bc = keep.tile([P, ROW_TILES * BLOCKS], BF16)
+        nc.sync.dma_start(out=sa_bc[:], in_=sq_a.rearrange("a b -> (a b)").partition_broadcast(P))
+        wa_raw = keep.tile([P, ROW_TILES, K], BF16)
+        nc.sync.dma_start(out=wa_raw[:], in_=wq_a.rearrange("(o p) i -> p o i", p=P))
+        x_loads = []
+        cos_loads = []
+        sin_loads = []
+
+        def load_x(c):
+            x_sb = x_pool.tile([P, LOAD_TILES, K], BF16)
+            nc.sync.dma_start(out=x_sb[:], in_=x_dram[:, c * LOAD_TILES : (c + 1) * LOAD_TILES, :])
+            x_loads.append(x_sb)
+
+        def load_tables(q):
+            tiles = slice(q * TABLE_TILES, (q + 1) * TABLE_TILES)
+            cos_sb = keep.tile([P, TABLE_TILES, ROPE], BF16, name="cos_%d" % q)
+            nc.sync.dma_start(out=cos_sb[:], in_=cos_dram[:, tiles, :])
+            cos_loads.append(cos_sb)
+            sin_sb = keep.tile([P, TABLE_TILES, ROPE], BF16, name="sin_%d" % q)
+            nc.sync.dma_start(out=sin_sb[:], in_=sin_dram[:, tiles, :])
+            sin_loads.append(sin_sb)
+
+        load_x(0)
+        sb_bc = keep.tile([P, ROW_TILES * BLOCKS], BF16)
+        nc.sync.dma_start(out=sb_bc[:], in_=sq_b.rearrange("a b -> (a b)").partition_broadcast(P))
+        wb_raw = keep.tile([P, ROW_TILES, K], BF16)
+        nc.sync.dma_start(out=wb_raw[:], in_=wq_b.rearrange("(o p) i -> p o i", p=P))
+        gain_bc = keep.tile([P, K], BF16)
+        nc.sync.dma_start(out=gain_bc[:], in_=q_ln_w.partition_broadcast(P))
+        for c in range(1, X_LOADS):
+            load_x(c)
+            if c % (TABLE_TILES // LOAD_TILES) == 1:
+                load_tables(c // (TABLE_TILES // LOAD_TILES))
+
+        ident = keep.tile([P, P], F32)
+        make_identity(nc, ident[:])
+        eps = keep.tile([P, 1], F32)
+        nc.vector.memset(eps[:], EPS)
+        warm = keep.tile([P, 1], F32)
+        nc.scalar.activation(out=warm[:], in_=eps[:], func=ACT.Sqrt)
+
+        def transpose_rows(bank, rows):
+            for j in range(UNIT_TILES):
+                row_words = rows[:, j, :].bitcast(F32)
+                for u in range(HALVES):
+                    nc.tensor.transpose(bank[:, j, u, :], row_words[:, u * P : (u + 1) * P], ident[:])
+
+        def scale_weight(engine, label, raw, factors):
+            scaled = keep.tile([P, ROW_TILES, K], BF16, name="scaled_" + label)
+            blocks = UNIT_TILES * BLOCKS
+            for m in range(ROW_TILES // UNIT_TILES):
+                rows = slice(m * UNIT_TILES, (m + 1) * UNIT_TILES)
+                engine.tensor_tensor(
+                    out=scaled[:, rows, :].rearrange("p o (b c) -> p (o b) c", c=P),
+                    in0=raw[:, rows, :].rearrange("p o (b c) -> p (o b) c", c=P),
+                    in1=factors[:, m * blocks : (m + 1) * blocks].unsqueeze(2).to_broadcast([P, blocks, P]),
+                    op=ALU.mult,
+                )
+            return scaled
+
+        def transpose_weight(label, scaled, column_order):
+            grouped = keep.tile([P, OUT, PACK], BF16, name="grouped_" + label, align_bytes=64)
+            columns = grouped[:].bitcast(F32).rearrange(column_order, o=ROW_TILES, c=2)
+            for m in range(ROW_TILES // UNIT_TILES):
+                bank = psum_words.tile([P, UNIT_TILES, HALVES, P], F32, tag="words_%d" % m)
+                transpose_rows(bank, scaled[:, m * UNIT_TILES : (m + 1) * UNIT_TILES, :])
+                for j in range(UNIT_TILES):
+                    nc.scalar.copy(
+                        out=columns[:, m * UNIT_TILES + j],
+                        in_=bank[:, j].rearrange("p u (c d) -> p c d u", c=2),
+                    )
+            return grouped
+
+        def quantise_weight(grouped, codes, scales):
+            nc.vector.quantize_mx(
+                out=codes[:].bitcast(FP8X4),
+                scales=scales[:],
+                in_=grouped[:].rearrange("p r t -> p (r t)"),
+            )
+
+        wa_codes = keep.tile([P, OUT], U32, align_bytes=64)
+        wa_scales = keep.tile([P, OUT], U8, align_bytes=64)
+        wb_codes = keep.tile([P, OUT], U32, align_bytes=64)
+        wb_scales = keep.tile([P, OUT], U8, align_bytes=64)
+        wa_scaled = scale_weight(nc.vector, "wa", wa_raw, sa_bc)
+        wa_grouped = transpose_weight("wa", wa_scaled, "p (o c d) u -> p o c d u")
+        quantise_weight(wa_grouped, wa_codes, wa_scales)
+        wb_scaled = scale_weight(nc.gpsimd, "wb", wb_raw, sb_bc)
+        wb_grouped = []
+
+        grouped_of = {}
+        codes_of = {}
+        lq_of = {}
+        sums_of = {}
+        h_of = {}
+        rope_of = {}
+        plain_of = {}
+
+        def transpose_unit(kind, n, rows):
+            bank = psum_words.tile([P, UNIT_TILES, HALVES, P], F32, tag="words_%d" % kind)
+            transpose_rows(bank, rows)
+            grouped = work.tile([P, UNIT_TILES, P, PACK], BF16, tag="grouped_%d" % kind, align_bytes=64)
+            nc.scalar.copy(out=grouped[:].bitcast(F32), in_=bank[:].rearrange("p j u r -> p j r u"))
+            grouped_of[(kind, n)] = grouped
+
+        def quantise_unit(kind, n):
+            grouped = grouped_of[(kind, n)]
+            codes = work.tile([P, UNIT_TILES * P], U32, tag="codes_%d" % kind, align_bytes=64)
+            scales = work.tile([P, UNIT_TILES * P], U8, tag="scales_%d" % kind, align_bytes=64)
+            nc.vector.quantize_mx(
+                out=codes[:].bitcast(FP8X4),
+                scales=scales[:],
+                in_=grouped[:].rearrange("p j r t -> p (j r t)"),
+            )
+            codes_of[(kind, n)] = (codes, scales)
+
+        def multiply(out, codes, scales, j, w_codes, w_scales, columns):
+            tokens = slice(j * P, (j + 1) * P)
+            nc.tensor.matmul_mx(
+                out=out,
+                lhsT=codes[:, tokens].bitcast(FP8X4),
+                lhsT_scale=scales[:, tokens],
+                rhs=w_codes[:, columns].bitcast(FP8X4),
+                rhs_scale=w_scales[:, columns],
+                start=True,
+                stop=True,
+            )
+
+        def first_matmul(n):
+            codes, scales = codes_of[(0, n)]
+            banks = []
+            for j in range(UNIT_TILES):
+                lq = psum_lq.tile([P, OUT], F32)
+                multiply(lq[:], codes, scales, j, wa_codes, wa_scales, slice(0, OUT))
+                banks.append(lq)
+            lq_of[n] = banks
+
+        def sum_squares(n):
+            sums = work.tile([P, UNIT_TILES], F32, tag="sums")
+            for j in range(UNIT_TILES):
+                squares = work.tile([P, OUT], BF16, tag="squares")
+                nc.scalar.activation(
+                    out=squares[:], in_=lq_of[n][j][:], func=ACT.Square, accum_out=sums[:, j : j + 1]
+                )
+            rms = work.tile([P, UNIT_TILES], F32, tag="rms")
+            nc.scalar.activation(out=rms[:], in_=sums[:], func=ACT.Sqrt, bias=eps[:], scale=1.0 / OUT)
+            sums_of[n] = rms
+
+        def normalise(n):
+            inverse = work.tile([P, UNIT_TILES], F32, tag="inverse")
+            nc.vector.reciprocal(out=inverse[:], in_=sums_of[n][:])
+            h = work.tile([P, UNIT_TILES, K], BF16, tag="h")
+            banks = lq_of[n]
+            for j in range(UNIT_TILES):
+                nc.vector.scalar_tensor_tensor(
+                    out=h[:, j, :],
+                    in0=banks[j][:],
+                    scalar=inverse[:, j : j + 1],
+                    in1=gain_bc[:],
+                    op0=ALU.mult,
+                    op1=ALU.mult,
+                )
+            h_of[n] = h
+
+        def second_matmul(n):
+            codes, scales = codes_of[(1, n)]
+            rope = psum_q.tile([P, UNIT_TILES, HEADS, ROPE], F32, tag="rope")
+            for j in range(UNIT_TILES):
+                multiply(
+                    rope[:, j].rearrange("p h d -> p (h d)"),
+                    codes, scales, j, wb_codes, wb_scales, slice(HEADS * NOPE, OUT),
+                )
+            rope_of[n] = rope
+            plain = psum_q.tile([P, UNIT_TILES, HEADS * NOPE], F32, tag="plain")
+            for j in range(UNIT_TILES):
+                multiply(plain[:, j, :], codes, scales, j, wb_codes, wb_scales, slice(0, HEADS * NOPE))
+            plain_of[n] = plain
+
+        def store_plain(n):
+            tiles = slice(n * UNIT_TILES, (n + 1) * UNIT_TILES)
+            nope_sb = results.tile([P, UNIT_TILES, HEADS * NOPE], F32, tag="nope")
+            nc.scalar.copy(out=nope_sb[:], in_=plain_of[n][:])
+            nc.sync.dma_start(out=nope_dram[:, tiles, :], in_=nope_sb[:])
+
+        def rotate(n):
+            tiles = slice(n * UNIT_TILES, (n + 1) * UNIT_TILES)
+            first = (n * UNIT_TILES) % TABLE_TILES
+            piece = (n * UNIT_TILES) // TABLE_TILES
+            shape = [P, UNIT_TILES, HEADS, ROPE]
+            cos_bc = cos_loads[piece][:, first : first + UNIT_TILES, :].unsqueeze(2).to_broadcast(shape)
+            sin_bc = sin_loads[piece][:, first : first + UNIT_TILES, :].unsqueeze(2).to_broadcast(shape)
+            low = slice(0, HALF)
+            high = slice(HALF, ROPE)
+            rope = rope_of[n]
+            straight = work.tile(shape, F32, tag="straight")
+            nc.vector.tensor_tensor(out=straight[:], in0=rope[:], in1=cos_bc, op=ALU.mult)
+            crossed = work.tile(shape, F32, tag="crossed")
+            nc.vector.tensor_tensor(
+                out=crossed[:, :, :, low], in0=rope[:, :, :, high], in1=sin_bc[:, :, :, low], op=ALU.mult
+            )
+            nc.vector.tensor_tensor(
+                out=crossed[:, :, :, high], in0=rope[:, :, :, low], in1=sin_bc[:, :, :, high], op=ALU.mult
+            )
+            rot_sb = results.tile(shape, F32, tag="rot")
+            nc.gpsimd.tensor_tensor(
+                out=rot_sb[:, :, :, low], in0=straight[:, :, :, low], in1=crossed[:, :, :, low], op=ALU.subtract
+            )
+            nc.gpsimd.tensor_tensor(
+                out=rot_sb[:, :, :, high], in0=straight[:, :, :, high], in1=crossed[:, :, :, high], op=ALU.add
+            )
+            nc.sync.dma_start(out=rot_dram[:, tiles, :], in_=rot_sb[:].rearrange("p t h d -> p t (h d)"))
+
+        def x_rows(n):
+            first = (n * UNIT_TILES) % LOAD_TILES
+            return x_loads[(n * UNIT_TILES) // LOAD_TILES][:, first : first + UNIT_TILES, :]
+
+        def active(n):
+            return 0 <= n < UNITS
+
+        for i in range(-X_LEAD, UNITS + Q_LAG):
+            if active(i):
+                quantise_unit(0, i)
+            if active(i - Q_LAG):
+                quantise_unit(1, i - Q_LAG)
+            if active(i):
+                first_matmul(i)
+            if active(i - Q_LAG):
+                second_matmul(i - Q_LAG)
+            if active(i):
+                sum_squares(i)
+            if active(i - 1):
+                normalise(i - 1)
+            if active(i - Q_LAG):
+                store_plain(i - Q_LAG)
+                rotate(i - Q_LAG)
+            if active(i + X_LEAD):
+                transpose_unit(0, i + X_LEAD, x_rows(i + X_LEAD))
+            if active(i - 1):
+                transpose_unit(1, i - 1, h_of[i - 1][:])
+            if i == WB_TRANSPOSE_ROUND:
+                wb_grouped.append(transpose_weight("wb", wb_scaled, "p (c o d) u -> p o c d u"))
+            if i == WB_QUANTISE_ROUND:
+                quantise_weight(wb_grouped[0], wb_codes, wb_scales)

@@ -26,12 +26,17 @@ HEADS = 4
 NOPE = 64
 ROPE = 64
 HALF = ROPE // 2
+LOW = slice(0, HALF)
+HIGH = slice(HALF, ROPE)
 OUT = HEADS * (NOPE + ROPE)
 ROW_TILES = OUT // P
 BLOCKS = K // P
 EPS = 1e-6
 X_LEAD = 2
 Q_LAG = 3
+ROTATE_LAG = Q_LAG + 1
+LQ_UNITS = 2
+PRODUCT_BUFS = 4
 WB_TRANSPOSE_ROUND = 1
 WB_QUANTISE_ROUND = 2
 
@@ -54,7 +59,7 @@ def tile_deepseekv3attention_pa_t_kernel(
         work = ctx.enter_context(tc.tile_pool(name="work", bufs=3))
         results = ctx.enter_context(tc.tile_pool(name="results", bufs=4))
         psum_words = ctx.enter_context(tc.psum_pool(name="psum_words", bufs=1))
-        psum_lq = ctx.enter_context(tc.psum_pool(name="psum_lq", bufs=2 * UNIT_TILES))
+        psum_lq = ctx.enter_context(tc.psum_pool(name="psum_lq", bufs=LQ_UNITS * UNIT_TILES))
         psum_q = ctx.enter_context(tc.psum_pool(name="psum_q", bufs=1))
         ctx.enter_context(tc.manual_schedule())
 
@@ -85,11 +90,12 @@ def tile_deepseekv3attention_pa_t_kernel(
         nc.sync.dma_start(out=sb_bc[:], in_=sq_b.rearrange("a b -> (a b)").partition_broadcast(P))
         wb_raw = keep.tile([P, ROW_TILES, K], BF16)
         nc.sync.dma_start(out=wb_raw[:], in_=wq_b.rearrange("(o p) i -> p o i", p=P))
+        load_x(1)
         gain_bc = keep.tile([P, K], BF16)
         nc.sync.dma_start(out=gain_bc[:], in_=q_ln_w.partition_broadcast(P))
-        for c in range(1, X_LOADS):
+        for c in range(2, X_LOADS):
             load_x(c)
-            if c % (TABLE_TILES // LOAD_TILES) == 1:
+            if c % (TABLE_TILES // LOAD_TILES) == 2:
                 load_tables(c // (TABLE_TILES // LOAD_TILES))
 
         ident = keep.tile([P, P], F32)
@@ -148,10 +154,14 @@ def tile_deepseekv3attention_pa_t_kernel(
         wb_scaled = scale_weight(nc.gpsimd, "wb", wb_raw, sb_bc)
         wb_grouped = []
 
+        words_of = {}
         grouped_of = {}
         codes_of = {}
         lq_of = {}
         sums_of = {}
+        rms_of = {}
+        inverse_of = {}
+        rot_of = {}
         h_of = {}
         rope_of = {}
         plain_of = {}
@@ -159,6 +169,10 @@ def tile_deepseekv3attention_pa_t_kernel(
         def transpose_unit(kind, n, rows):
             bank = psum_words.tile([P, UNIT_TILES, HALVES, P], F32, tag="words_%d" % kind)
             transpose_rows(bank, rows)
+            words_of[(kind, n)] = bank
+
+        def group_unit(kind, n):
+            bank = words_of[(kind, n)]
             grouped = work.tile([P, UNIT_TILES, P, PACK], BF16, tag="grouped_%d" % kind, align_bytes=64)
             nc.scalar.copy(out=grouped[:].bitcast(F32), in_=bank[:].rearrange("p j u r -> p j r u"))
             grouped_of[(kind, n)] = grouped
@@ -202,13 +216,20 @@ def tile_deepseekv3attention_pa_t_kernel(
                 nc.scalar.activation(
                     out=squares[:], in_=lq_of[n][j][:], func=ACT.Square, accum_out=sums[:, j : j + 1]
                 )
+            sums_of[n] = sums
+
+        def root(n):
             rms = work.tile([P, UNIT_TILES], F32, tag="rms")
-            nc.scalar.activation(out=rms[:], in_=sums[:], func=ACT.Sqrt, bias=eps[:], scale=1.0 / OUT)
-            sums_of[n] = rms
+            nc.scalar.activation(out=rms[:], in_=sums_of[n][:], func=ACT.Sqrt, bias=eps[:], scale=1.0 / OUT)
+            rms_of[n] = rms
+
+        def invert(n):
+            inverse = work.tile([P, UNIT_TILES], F32, tag="inverse")
+            nc.vector.reciprocal(out=inverse[:], in_=rms_of[n][:])
+            inverse_of[n] = inverse
 
         def normalise(n):
-            inverse = work.tile([P, UNIT_TILES], F32, tag="inverse")
-            nc.vector.reciprocal(out=inverse[:], in_=sums_of[n][:])
+            inverse = inverse_of[n]
             h = work.tile([P, UNIT_TILES, K], BF16, tag="h")
             banks = lq_of[n]
             for j in range(UNIT_TILES):
@@ -222,7 +243,7 @@ def tile_deepseekv3attention_pa_t_kernel(
                 )
             h_of[n] = h
 
-        def second_matmul(n):
+        def second_matmul_rotated(n):
             codes, scales = codes_of[(1, n)]
             rope = psum_q.tile([P, UNIT_TILES, HEADS, ROPE], F32, tag="rope")
             for j in range(UNIT_TILES):
@@ -231,6 +252,9 @@ def tile_deepseekv3attention_pa_t_kernel(
                     codes, scales, j, wb_codes, wb_scales, slice(HEADS * NOPE, OUT),
                 )
             rope_of[n] = rope
+
+        def second_matmul_plain(n):
+            codes, scales = codes_of[(1, n)]
             plain = psum_q.tile([P, UNIT_TILES, HEADS * NOPE], F32, tag="plain")
             for j in range(UNIT_TILES):
                 multiply(plain[:, j, :], codes, scales, j, wb_codes, wb_scales, slice(0, HEADS * NOPE))
@@ -242,33 +266,32 @@ def tile_deepseekv3attention_pa_t_kernel(
             nc.scalar.copy(out=nope_sb[:], in_=plain_of[n][:])
             nc.sync.dma_start(out=nope_dram[:, tiles, :], in_=nope_sb[:])
 
-        def rotate(n):
-            tiles = slice(n * UNIT_TILES, (n + 1) * UNIT_TILES)
+        def rotate(n, here, there, sum_op):
             first = (n * UNIT_TILES) % TABLE_TILES
             piece = (n * UNIT_TILES) // TABLE_TILES
             shape = [P, UNIT_TILES, HEADS, ROPE]
             cos_bc = cos_loads[piece][:, first : first + UNIT_TILES, :].unsqueeze(2).to_broadcast(shape)
             sin_bc = sin_loads[piece][:, first : first + UNIT_TILES, :].unsqueeze(2).to_broadcast(shape)
-            low = slice(0, HALF)
-            high = slice(HALF, ROPE)
             rope = rope_of[n]
-            straight = work.tile(shape, F32, tag="straight")
-            nc.vector.tensor_tensor(out=straight[:], in0=rope[:], in1=cos_bc, op=ALU.mult)
-            crossed = work.tile(shape, F32, tag="crossed")
+            half_shape = [P, UNIT_TILES, HEADS, HALF]
+            straight = work.tile(half_shape, F32, tag="straight", bufs=PRODUCT_BUFS)
             nc.vector.tensor_tensor(
-                out=crossed[:, :, :, low], in0=rope[:, :, :, high], in1=sin_bc[:, :, :, low], op=ALU.mult
+                out=straight[:], in0=rope[:, :, :, here], in1=cos_bc[:, :, :, here], op=ALU.mult
             )
+            crossed = work.tile(half_shape, F32, tag="crossed", bufs=PRODUCT_BUFS)
             nc.vector.tensor_tensor(
-                out=crossed[:, :, :, high], in0=rope[:, :, :, low], in1=sin_bc[:, :, :, high], op=ALU.mult
+                out=crossed[:], in0=rope[:, :, :, there], in1=sin_bc[:, :, :, here], op=ALU.mult
             )
-            rot_sb = results.tile(shape, F32, tag="rot")
-            nc.gpsimd.tensor_tensor(
-                out=rot_sb[:, :, :, low], in0=straight[:, :, :, low], in1=crossed[:, :, :, low], op=ALU.subtract
-            )
-            nc.gpsimd.tensor_tensor(
-                out=rot_sb[:, :, :, high], in0=straight[:, :, :, high], in1=crossed[:, :, :, high], op=ALU.add
-            )
-            nc.sync.dma_start(out=rot_dram[:, tiles, :], in_=rot_sb[:].rearrange("p t h d -> p t (h d)"))
+            nc.gpsimd.tensor_tensor(out=rot_of[n][:, :, :, here], in0=straight[:], in1=crossed[:], op=sum_op)
+
+        def rotate_low(n):
+            rot_of[n] = results.tile([P, UNIT_TILES, HEADS, ROPE], F32, name="rot_sb", tag="rot")
+            rotate(n, LOW, HIGH, ALU.subtract)
+
+        def rotate_high(n):
+            rotate(n, HIGH, LOW, ALU.add)
+            tiles = slice(n * UNIT_TILES, (n + 1) * UNIT_TILES)
+            nc.sync.dma_start(out=rot_dram[:, tiles, :], in_=rot_of[n][:].rearrange("p t h d -> p t (h d)"))
 
         def x_rows(n):
             first = (n * UNIT_TILES) % LOAD_TILES
@@ -277,26 +300,38 @@ def tile_deepseekv3attention_pa_t_kernel(
         def active(n):
             return 0 <= n < UNITS
 
-        for i in range(-X_LEAD, UNITS + Q_LAG):
-            if active(i):
-                quantise_unit(0, i)
+        for i in range(-X_LEAD, UNITS + ROTATE_LAG):
             if active(i - Q_LAG):
                 quantise_unit(1, i - Q_LAG)
             if active(i):
-                first_matmul(i)
-            if active(i - Q_LAG):
-                second_matmul(i - Q_LAG)
-            if active(i):
-                sum_squares(i)
+                quantise_unit(0, i)
+            if active(i - ROTATE_LAG):
+                rotate_low(i - ROTATE_LAG)
+            if active(i - 1):
+                invert(i - 1)
+            if active(i - ROTATE_LAG):
+                rotate_high(i - ROTATE_LAG)
             if active(i - 1):
                 normalise(i - 1)
+            if active(i):
+                first_matmul(i)
             if active(i - Q_LAG):
-                store_plain(i - Q_LAG)
-                rotate(i - Q_LAG)
+                second_matmul_plain(i - Q_LAG)
+                second_matmul_rotated(i - Q_LAG)
             if active(i + X_LEAD):
                 transpose_unit(0, i + X_LEAD, x_rows(i + X_LEAD))
             if active(i - 1):
                 transpose_unit(1, i - 1, h_of[i - 1][:])
+            if active(i):
+                sum_squares(i)
+            if active(i - Q_LAG):
+                store_plain(i - Q_LAG)
+            if active(i):
+                root(i)
+            if active(i + X_LEAD):
+                group_unit(0, i + X_LEAD)
+            if active(i - 1):
+                group_unit(1, i - 1)
             if i == WB_TRANSPOSE_ROUND:
                 wb_grouped.append(transpose_weight("wb", wb_scaled, "p (c o d) u -> p o c d u"))
             if i == WB_QUANTISE_ROUND:

@@ -19,9 +19,8 @@ TOKENS = 8192
 TILES = TOKENS // P
 UNIT_TILES = 2
 UNITS = TILES // UNIT_TILES
-LOAD_TILES = 4
-X_LOADS = TILES // LOAD_TILES
-TABLE_TILES = 16
+TABLE_UNITS = 8
+TABLE_TILES = TABLE_UNITS * UNIT_TILES
 HEADS = 4
 NOPE = 64
 ROPE = 64
@@ -32,7 +31,9 @@ OUT = HEADS * (NOPE + ROPE)
 ROW_TILES = OUT // P
 BLOCKS = K // P
 EPS = 1e-6
+WEIGHT_HALVES = ROW_TILES // UNIT_TILES
 X_LEAD = 2
+assert X_LEAD == WEIGHT_HALVES
 Q_LAG = 3
 ROTATE_LAG = Q_LAG + 1
 LQ_UNITS = 2
@@ -55,25 +56,27 @@ def tile_deepseekv3attention_pa_t_kernel(
 
     with ExitStack() as ctx:
         keep = ctx.enter_context(tc.tile_pool(name="keep", bufs=1))
-        x_pool = ctx.enter_context(tc.tile_pool(name="x", bufs=X_LOADS))
+        x_pool = ctx.enter_context(tc.tile_pool(name="x", bufs=UNITS))
         work = ctx.enter_context(tc.tile_pool(name="work", bufs=3))
         results = ctx.enter_context(tc.tile_pool(name="results", bufs=4))
-        psum_words = ctx.enter_context(tc.psum_pool(name="psum_words", bufs=1))
         psum_lq = ctx.enter_context(tc.psum_pool(name="psum_lq", bufs=LQ_UNITS * UNIT_TILES))
-        psum_q = ctx.enter_context(tc.psum_pool(name="psum_q", bufs=1))
+        psum_own = ctx.enter_context(tc.psum_pool(name="psum_own", bufs=1))
+        psum_turns = ctx.enter_context(tc.psum_pool(name="psum_turns", bufs=2))
         ctx.enter_context(tc.manual_schedule())
 
         sa_bc = keep.tile([P, ROW_TILES * BLOCKS], BF16)
         nc.sync.dma_start(out=sa_bc[:], in_=sq_a.rearrange("a b -> (a b)").partition_broadcast(P))
         wa_raw = keep.tile([P, ROW_TILES, K], BF16)
-        nc.sync.dma_start(out=wa_raw[:], in_=wq_a.rearrange("(o p) i -> p o i", p=P))
+        wa_dram = wq_a.rearrange("(o p) i -> p o i", p=P)
+        for o in range(ROW_TILES):
+            nc.sync.dma_start(out=wa_raw[:, o, :], in_=wa_dram[:, o, :])
         x_loads = []
         cos_loads = []
         sin_loads = []
 
-        def load_x(c):
-            x_sb = x_pool.tile([P, LOAD_TILES, K], BF16)
-            nc.sync.dma_start(out=x_sb[:], in_=x_dram[:, c * LOAD_TILES : (c + 1) * LOAD_TILES, :])
+        def load_x(n):
+            x_sb = x_pool.tile([P, UNIT_TILES, K], BF16)
+            nc.sync.dma_start(out=x_sb[:], in_=x_dram[:, n * UNIT_TILES : (n + 1) * UNIT_TILES, :])
             x_loads.append(x_sb)
 
         def load_tables(q):
@@ -90,13 +93,14 @@ def tile_deepseekv3attention_pa_t_kernel(
         nc.sync.dma_start(out=sb_bc[:], in_=sq_b.rearrange("a b -> (a b)").partition_broadcast(P))
         wb_raw = keep.tile([P, ROW_TILES, K], BF16)
         nc.sync.dma_start(out=wb_raw[:], in_=wq_b.rearrange("(o p) i -> p o i", p=P))
-        load_x(1)
+        for n in range(1, ROTATE_LAG):
+            load_x(n)
         gain_bc = keep.tile([P, K], BF16)
         nc.sync.dma_start(out=gain_bc[:], in_=q_ln_w.partition_broadcast(P))
-        for c in range(2, X_LOADS):
-            load_x(c)
-            if c % (TABLE_TILES // LOAD_TILES) == 2:
-                load_tables(c // (TABLE_TILES // LOAD_TILES))
+        for n in range(ROTATE_LAG, UNITS):
+            load_x(n)
+            if n % TABLE_UNITS == ROTATE_LAG:
+                load_tables(n // TABLE_UNITS)
 
         ident = keep.tile([P, P], F32)
         make_identity(nc, ident[:])
@@ -105,54 +109,50 @@ def tile_deepseekv3attention_pa_t_kernel(
         warm = keep.tile([P, 1], F32)
         nc.scalar.activation(out=warm[:], in_=eps[:], func=ACT.Sqrt)
 
-        def transpose_rows(bank, rows):
+        def transpose_rows(kind, rows):
+            if kind == 0:
+                bank = psum_turns.tile([P, UNIT_TILES, HALVES, P], F32, tag="turns")
+            else:
+                bank = psum_own.tile([P, UNIT_TILES, HALVES, P], F32, tag="words_h")
             for j in range(UNIT_TILES):
                 row_words = rows[:, j, :].bitcast(F32)
                 for u in range(HALVES):
                     nc.tensor.transpose(bank[:, j, u, :], row_words[:, u * P : (u + 1) * P], ident[:])
+            return bank
 
         def scale_weight(engine, label, raw, factors):
             scaled = keep.tile([P, ROW_TILES, K], BF16, name="scaled_" + label)
-            blocks = UNIT_TILES * BLOCKS
-            for m in range(ROW_TILES // UNIT_TILES):
-                rows = slice(m * UNIT_TILES, (m + 1) * UNIT_TILES)
+            for o in range(ROW_TILES):
                 engine.tensor_tensor(
-                    out=scaled[:, rows, :].rearrange("p o (b c) -> p (o b) c", c=P),
-                    in0=raw[:, rows, :].rearrange("p o (b c) -> p (o b) c", c=P),
-                    in1=factors[:, m * blocks : (m + 1) * blocks].unsqueeze(2).to_broadcast([P, blocks, P]),
+                    out=scaled[:, o, :].rearrange("p (b c) -> p b c", c=P),
+                    in0=raw[:, o, :].rearrange("p (b c) -> p b c", c=P),
+                    in1=factors[:, o * BLOCKS : (o + 1) * BLOCKS].unsqueeze(2).to_broadcast([P, BLOCKS, P]),
                     op=ALU.mult,
                 )
             return scaled
 
-        def transpose_weight(label, scaled, column_order):
-            grouped = keep.tile([P, OUT, PACK], BF16, name="grouped_" + label, align_bytes=64)
+        def transpose_weight(grouped, scaled, column_order, m):
             columns = grouped[:].bitcast(F32).rearrange(column_order, o=ROW_TILES, c=2)
-            for m in range(ROW_TILES // UNIT_TILES):
-                bank = psum_words.tile([P, UNIT_TILES, HALVES, P], F32, tag="words_%d" % m)
-                transpose_rows(bank, scaled[:, m * UNIT_TILES : (m + 1) * UNIT_TILES, :])
-                for j in range(UNIT_TILES):
-                    nc.scalar.copy(
-                        out=columns[:, m * UNIT_TILES + j],
-                        in_=bank[:, j].rearrange("p u (c d) -> p c d u", c=2),
-                    )
-            return grouped
+            bank = transpose_rows(m, scaled[:, m * UNIT_TILES : (m + 1) * UNIT_TILES, :])
+            for j in range(UNIT_TILES):
+                nc.scalar.copy(
+                    out=columns[:, m * UNIT_TILES + j],
+                    in_=bank[:, j].rearrange("p u (c d) -> p c d u", c=2),
+                )
 
-        def quantise_weight(grouped, codes, scales):
+        def quantise_weight(grouped, codes, scales, columns):
             nc.vector.quantize_mx(
-                out=codes[:].bitcast(FP8X4),
-                scales=scales[:],
-                in_=grouped[:].rearrange("p r t -> p (r t)"),
+                out=codes[:, columns].bitcast(FP8X4),
+                scales=scales[:, columns],
+                in_=grouped[:, columns, :].rearrange("p r t -> p (r t)"),
             )
 
+        wa_grouped = keep.tile([P, OUT, PACK], BF16, align_bytes=64)
         wa_codes = keep.tile([P, OUT], U32, align_bytes=64)
         wa_scales = keep.tile([P, OUT], U8, align_bytes=64)
+        wb_grouped = keep.tile([P, OUT, PACK], BF16, align_bytes=64)
         wb_codes = keep.tile([P, OUT], U32, align_bytes=64)
         wb_scales = keep.tile([P, OUT], U8, align_bytes=64)
-        wa_scaled = scale_weight(nc.vector, "wa", wa_raw, sa_bc)
-        wa_grouped = transpose_weight("wa", wa_scaled, "p (o c d) u -> p o c d u")
-        quantise_weight(wa_grouped, wa_codes, wa_scales)
-        wb_scaled = scale_weight(nc.gpsimd, "wb", wb_raw, sb_bc)
-        wb_grouped = []
 
         words_of = {}
         grouped_of = {}
@@ -167,9 +167,7 @@ def tile_deepseekv3attention_pa_t_kernel(
         plain_of = {}
 
         def transpose_unit(kind, n, rows):
-            bank = psum_words.tile([P, UNIT_TILES, HALVES, P], F32, tag="words_%d" % kind)
-            transpose_rows(bank, rows)
-            words_of[(kind, n)] = bank
+            words_of[(kind, n)] = transpose_rows(kind, rows)
 
         def group_unit(kind, n):
             bank = words_of[(kind, n)]
@@ -245,7 +243,7 @@ def tile_deepseekv3attention_pa_t_kernel(
 
         def second_matmul_rotated(n):
             codes, scales = codes_of[(1, n)]
-            rope = psum_q.tile([P, UNIT_TILES, HEADS, ROPE], F32, tag="rope")
+            rope = psum_turns.tile([P, UNIT_TILES, HEADS, ROPE], F32, tag="turns")
             for j in range(UNIT_TILES):
                 multiply(
                     rope[:, j].rearrange("p h d -> p (h d)"),
@@ -255,7 +253,7 @@ def tile_deepseekv3attention_pa_t_kernel(
 
         def second_matmul_plain(n):
             codes, scales = codes_of[(1, n)]
-            plain = psum_q.tile([P, UNIT_TILES, HEADS * NOPE], F32, tag="plain")
+            plain = psum_own.tile([P, UNIT_TILES, HEADS * NOPE], F32, tag="plain")
             for j in range(UNIT_TILES):
                 multiply(plain[:, j, :], codes, scales, j, wb_codes, wb_scales, slice(0, HEADS * NOPE))
             plain_of[n] = plain
@@ -293,14 +291,18 @@ def tile_deepseekv3attention_pa_t_kernel(
             tiles = slice(n * UNIT_TILES, (n + 1) * UNIT_TILES)
             nc.sync.dma_start(out=rot_dram[:, tiles, :], in_=rot_of[n][:].rearrange("p t h d -> p t (h d)"))
 
-        def x_rows(n):
-            first = (n * UNIT_TILES) % LOAD_TILES
-            return x_loads[(n * UNIT_TILES) // LOAD_TILES][:, first : first + UNIT_TILES, :]
+        wa_scaled = scale_weight(nc.vector, "wa", wa_raw, sa_bc)
+        for m in range(WEIGHT_HALVES):
+            transpose_weight(wa_grouped, wa_scaled, "p (o c d) u -> p o c d u", m)
+            quantise_weight(wa_grouped, wa_codes, wa_scales, slice(m * UNIT_TILES * P, (m + 1) * UNIT_TILES * P))
+            transpose_unit(0, m, x_loads[m][:])
+            group_unit(0, m)
+        wb_scaled = scale_weight(nc.gpsimd, "wb", wb_raw, sb_bc)
 
         def active(n):
             return 0 <= n < UNITS
 
-        for i in range(-X_LEAD, UNITS + ROTATE_LAG):
+        for i in range(UNITS + ROTATE_LAG):
             if active(i - Q_LAG):
                 quantise_unit(1, i - Q_LAG)
             if active(i):
@@ -319,7 +321,7 @@ def tile_deepseekv3attention_pa_t_kernel(
                 second_matmul_plain(i - Q_LAG)
                 second_matmul_rotated(i - Q_LAG)
             if active(i + X_LEAD):
-                transpose_unit(0, i + X_LEAD, x_rows(i + X_LEAD))
+                transpose_unit(0, i + X_LEAD, x_loads[i + X_LEAD][:])
             if active(i - 1):
                 transpose_unit(1, i - 1, h_of[i - 1][:])
             if active(i):
@@ -333,6 +335,7 @@ def tile_deepseekv3attention_pa_t_kernel(
             if active(i - 1):
                 group_unit(1, i - 1)
             if i == WB_TRANSPOSE_ROUND:
-                wb_grouped.append(transpose_weight("wb", wb_scaled, "p (c o d) u -> p o c d u"))
+                for m in range(WEIGHT_HALVES):
+                    transpose_weight(wb_grouped, wb_scaled, "p (c o d) u -> p o c d u", m)
             if i == WB_QUANTISE_ROUND:
-                quantise_weight(wb_grouped[0], wb_codes, wb_scales)
+                quantise_weight(wb_grouped, wb_codes, wb_scales, slice(0, OUT))

@@ -303,12 +303,12 @@ def tile_deepseekv3attention_pa_t_kernel(
             return 0 <= n < UNITS
 
         for i in range(UNITS + ROTATE_LAG):
-            if active(i - Q_LAG):
-                quantise_unit(1, i - Q_LAG)
-            if active(i):
-                quantise_unit(0, i)
             if active(i - ROTATE_LAG):
                 rotate_low(i - ROTATE_LAG)
+            if active(i):
+                quantise_unit(0, i)
+            if active(i - Q_LAG):
+                quantise_unit(1, i - Q_LAG)
             if active(i - 1):
                 invert(i - 1)
             if active(i - ROTATE_LAG):
@@ -318,8 +318,8 @@ def tile_deepseekv3attention_pa_t_kernel(
             if active(i):
                 first_matmul(i)
             if active(i - Q_LAG):
-                second_matmul_plain(i - Q_LAG)
                 second_matmul_rotated(i - Q_LAG)
+                second_matmul_plain(i - Q_LAG)
             if active(i + X_LEAD):
                 transpose_unit(0, i + X_LEAD, x_loads[i + X_LEAD][:])
             if active(i - 1):

from contextlib import ExitStack

import concourse.mybir as mybir
from concourse.masks import make_identity

BF16 = mybir.dt.bfloat16
F32 = mybir.dt.float32
U32 = mybir.dt.uint32
U8 = mybir.dt.uint8
FP8X4 = mybir.dt.float8_e4m3fn_x4
ACT = mybir.ActivationFunctionType
ALU = mybir.AluOpType

P = 128
PACK = 4
K = P * PACK
HALVES = 2
TOKENS = 8192
TILES = TOKENS // P
UNIT_TILES = 2
UNITS = TILES // UNIT_TILES
TABLE_UNITS = 8
TABLE_TILES = TABLE_UNITS * UNIT_TILES
HEADS = 4
NOPE = 64
ROPE = 64
HALF = ROPE // 2
LOW = slice(0, HALF)
HIGH = slice(HALF, ROPE)
OUT = HEADS * (NOPE + ROPE)
ROW_TILES = OUT // P
BLOCKS = K // P
EPS = 1e-6
WEIGHT_HALVES = ROW_TILES // UNIT_TILES
X_LEAD = 2
assert X_LEAD == WEIGHT_HALVES
Q_LAG = 3
ROTATE_LAG = Q_LAG + 1
LQ_UNITS = 2
PRODUCT_BUFS = 4
WB_TRANSPOSE_ROUND = 1
WB_QUANTISE_ROUND = 2

FLOPS = 2 * 2 * TOKENS * K * OUT


def tile_deepseekv3attention_pa_t_kernel(
    tc, hidden_states, cos, sin, wq_a, sq_a, wq_b, sq_b, q_ln_w, out_0, out_1
):
    nc = tc.nc
    x_dram = hidden_states.rearrange("(p t) k -> p t k", t=TILES)
    cos_dram = cos.rearrange("(p t) d -> p t d", t=TILES)
    sin_dram = sin.rearrange("(p t) d -> p t d", t=TILES)
    nope_dram = out_0.rearrange("(p t) h d -> p t (h d)", t=TILES)
    rot_dram = out_1.rearrange("(p t) h d -> p t (h d)", t=TILES)

    with ExitStack() as ctx:
        keep = ctx.enter_context(tc.tile_pool(name="keep", bufs=1))
        x_pool = ctx.enter_context(tc.tile_pool(name="x", bufs=UNITS))
        work = ctx.enter_context(tc.tile_pool(name="work", bufs=3))
        results = ctx.enter_context(tc.tile_pool(name="results", bufs=4))
        psum_lq = ctx.enter_context(tc.psum_pool(name="psum_lq", bufs=LQ_UNITS * UNIT_TILES))
        psum_own = ctx.enter_context(tc.psum_pool(name="psum_own", bufs=1))
        psum_turns = ctx.enter_context(tc.psum_pool(name="psum_turns", bufs=2))
        ctx.enter_context(tc.manual_schedule())

        sa_bc = keep.tile([P, ROW_TILES * BLOCKS], BF16)
        nc.sync.dma_start(out=sa_bc[:], in_=sq_a.rearrange("a b -> (a b)").partition_broadcast(P))
        wa_raw = keep.tile([P, ROW_TILES, K], BF16)
        wa_dram = wq_a.rearrange("(o p) i -> p o i", p=P)
        for o in range(ROW_TILES):
            nc.sync.dma_start(out=wa_raw[:, o, :], in_=wa_dram[:, o, :])
        x_loads = []
        cos_loads = []
        sin_loads = []

        def load_x(n):
            x_sb = x_pool.tile([P, UNIT_TILES, K], BF16)
            nc.sync.dma_start(out=x_sb[:], in_=x_dram[:, n * UNIT_TILES : (n + 1) * UNIT_TILES, :])
            x_loads.append(x_sb)

        def load_tables(q):
            tiles = slice(q * TABLE_TILES, (q + 1) * TABLE_TILES)
            cos_sb = keep.tile([P, TABLE_TILES, ROPE], BF16, name="cos_%d" % q)
            nc.sync.dma_start(out=cos_sb[:], in_=cos_dram[:, tiles, :])
            cos_loads.append(cos_sb)
            sin_sb = keep.tile([P, TABLE_TILES, ROPE], BF16, name="sin_%d" % q)
            nc.sync.dma_start(out=sin_sb[:], in_=sin_dram[:, tiles, :])
            sin_loads.append(sin_sb)

        load_x(0)
        sb_bc = keep.tile([P, ROW_TILES * BLOCKS], BF16)
        nc.sync.dma_start(out=sb_bc[:], in_=sq_b.rearrange("a b -> (a b)").partition_broadcast(P))
        wb_raw = keep.tile([P, ROW_TILES, K], BF16)
        nc.sync.dma_start(out=wb_raw[:], in_=wq_b.rearrange("(o p) i -> p o i", p=P))
        for n in range(1, ROTATE_LAG):
            load_x(n)
        gain_bc = keep.tile([P, K], BF16)
        nc.sync.dma_start(out=gain_bc[:], in_=q_ln_w.partition_broadcast(P))
        for n in range(ROTATE_LAG, UNITS):
            load_x(n)
            if n % TABLE_UNITS == ROTATE_LAG:
                load_tables(n // TABLE_UNITS)

        ident = keep.tile([P, P], F32)
        make_identity(nc, ident[:])
        eps = keep.tile([P, 1], F32)
        nc.vector.memset(eps[:], EPS)
        warm = keep.tile([P, 1], F32)
        nc.scalar.activation(out=warm[:], in_=eps[:], func=ACT.Sqrt)

        def transpose_rows(kind, rows):
            if kind == 0:
                bank = psum_turns.tile([P, UNIT_TILES, HALVES, P], F32, tag="turns")
            else:
                bank = psum_own.tile([P, UNIT_TILES, HALVES, P], F32, tag="words_h")
            for j in range(UNIT_TILES):
                row_words = rows[:, j, :].bitcast(F32)
                for u in range(HALVES):
                    nc.tensor.transpose(bank[:, j, u, :], row_words[:, u * P : (u + 1) * P], ident[:])
            return bank

        def scale_weight(engine, label, raw, factors):
            scaled = keep.tile([P, ROW_TILES, K], BF16, name="scaled_" + label)
            for o in range(ROW_TILES):
                engine.tensor_tensor(
                    out=scaled[:, o, :].rearrange("p (b c) -> p b c", c=P),
                    in0=raw[:, o, :].rearrange("p (b c) -> p b c", c=P),
                    in1=factors[:, o * BLOCKS : (o + 1) * BLOCKS].unsqueeze(2).to_broadcast([P, BLOCKS, P]),
                    op=ALU.mult,
                )
            return scaled

        def transpose_weight(grouped, scaled, column_order, m):
            columns = grouped[:].bitcast(F32).rearrange(column_order, o=ROW_TILES, c=2)
            bank = transpose_rows(m, scaled[:, m * UNIT_TILES : (m + 1) * UNIT_TILES, :])
            for j in range(UNIT_TILES):
                nc.scalar.copy(
                    out=columns[:, m * UNIT_TILES + j],
                    in_=bank[:, j].rearrange("p u (c d) -> p c d u", c=2),
                )

        def quantise_weight(grouped, codes, scales, columns):
            nc.vector.quantize_mx(
                out=codes[:, columns].bitcast(FP8X4),
                scales=scales[:, columns],
                in_=grouped[:, columns, :].rearrange("p r t -> p (r t)"),
            )

        wa_grouped = keep.tile([P, OUT, PACK], BF16, align_bytes=64)
        wa_codes = keep.tile([P, OUT], U32, align_bytes=64)
        wa_scales = keep.tile([P, OUT], U8, align_bytes=64)
        wb_grouped = keep.tile([P, OUT, PACK], BF16, align_bytes=64)
        wb_codes = keep.tile([P, OUT], U32, align_bytes=64)
        wb_scales = keep.tile([P, OUT], U8, align_bytes=64)

        words_of = {}
        grouped_of = {}
        codes_of = {}
        lq_of = {}
        sums_of = {}
        rms_of = {}
        inverse_of = {}
        rot_of = {}
        h_of = {}
        rope_of = {}
        plain_of = {}

        def transpose_unit(kind, n, rows):
            words_of[(kind, n)] = transpose_rows(kind, rows)

        def group_unit(kind, n):
            bank = words_of[(kind, n)]
            grouped = work.tile([P, UNIT_TILES, P, PACK], BF16, tag="grouped_%d" % kind, align_bytes=64)
            nc.scalar.copy(out=grouped[:].bitcast(F32), in_=bank[:].rearrange("p j u r -> p j r u"))
            grouped_of[(kind, n)] = grouped

        def quantise_unit(kind, n):
            grouped = grouped_of[(kind, n)]
            codes = work.tile([P, UNIT_TILES * P], U32, tag="codes_%d" % kind, align_bytes=64)
            scales = work.tile([P, UNIT_TILES * P], U8, tag="scales_%d" % kind, align_bytes=64)
            nc.vector.quantize_mx(
                out=codes[:].bitcast(FP8X4),
                scales=scales[:],
                in_=grouped[:].rearrange("p j r t -> p (j r t)"),
            )
            codes_of[(kind, n)] = (codes, scales)

        def multiply(out, codes, scales, j, w_codes, w_scales, columns):
            tokens = slice(j * P, (j + 1) * P)
            nc.tensor.matmul_mx(
                out=out,
                lhsT=codes[:, tokens].bitcast(FP8X4),
                lhsT_scale=scales[:, tokens],
                rhs=w_codes[:, columns].bitcast(FP8X4),
                rhs_scale=w_scales[:, columns],
                start=True,
                stop=True,
            )

        def first_matmul(n):
            codes, scales = codes_of[(0, n)]
            banks = []
            for j in range(UNIT_TILES):
                lq = psum_lq.tile([P, OUT], F32)
                multiply(lq[:], codes, scales, j, wa_codes, wa_scales, slice(0, OUT))
                banks.append(lq)
            lq_of[n] = banks

        def sum_squares(n):
            sums = work.tile([P, UNIT_TILES], F32, tag="sums")
            for j in range(UNIT_TILES):
                squares = work.tile([P, OUT], BF16, tag="squares")
                nc.scalar.activation(
                    out=squares[:], in_=lq_of[n][j][:], func=ACT.Square, accum_out=sums[:, j : j + 1]
                )
            sums_of[n] = sums

        def root(n):
            rms = work.tile([P, UNIT_TILES], F32, tag="rms")
            nc.scalar.activation(out=rms[:], in_=sums_of[n][:], func=ACT.Sqrt, bias=eps[:], scale=1.0 / OUT)
            rms_of[n] = rms

        def invert(n):
            inverse = work.tile([P, UNIT_TILES], F32, tag="inverse")
            nc.vector.reciprocal(out=inverse[:], in_=rms_of[n][:])
            inverse_of[n] = inverse

        def normalise(n):
            inverse = inverse_of[n]
            h = work.tile([P, UNIT_TILES, K], BF16, tag="h")
            banks = lq_of[n]
            for j in range(UNIT_TILES):
                nc.vector.scalar_tensor_tensor(
                    out=h[:, j, :],
                    in0=banks[j][:],
                    scalar=inverse[:, j : j + 1],
                    in1=gain_bc[:],
                    op0=ALU.mult,
                    op1=ALU.mult,
                )
            h_of[n] = h

        def second_matmul_rotated(n):
            codes, scales = codes_of[(1, n)]
            rope = psum_turns.tile([P, UNIT_TILES, HEADS, ROPE], F32, tag="turns")
            for j in range(UNIT_TILES):
                multiply(
                    rope[:, j].rearrange("p h d -> p (h d)"),
                    codes, scales, j, wb_codes, wb_scales, slice(HEADS * NOPE, OUT),
                )
            rope_of[n] = rope

        def second_matmul_plain(n):
            codes, scales = codes_of[(1, n)]
            plain = psum_own.tile([P, UNIT_TILES, HEADS * NOPE], F32, tag="plain")
            for j in range(UNIT_TILES):
                multiply(plain[:, j, :], codes, scales, j, wb_codes, wb_scales, slice(0, HEADS * NOPE))
            plain_of[n] = plain

        def store_plain(n):
            tiles = slice(n * UNIT_TILES, (n + 1) * UNIT_TILES)
            nope_sb = results.tile([P, UNIT_TILES, HEADS * NOPE], F32, tag="nope")
            nc.scalar.copy(out=nope_sb[:], in_=plain_of[n][:])
            nc.sync.dma_start(out=nope_dram[:, tiles, :], in_=nope_sb[:])

        def rotate(n, here, there, sum_op):
            first = (n * UNIT_TILES) % TABLE_TILES
            piece = (n * UNIT_TILES) // TABLE_TILES
            shape = [P, UNIT_TILES, HEADS, ROPE]
            cos_bc = cos_loads[piece][:, first : first + UNIT_TILES, :].unsqueeze(2).to_broadcast(shape)
            sin_bc = sin_loads[piece][:, first : first + UNIT_TILES, :].unsqueeze(2).to_broadcast(shape)
            rope = rope_of[n]
            half_shape = [P, UNIT_TILES, HEADS, HALF]
            straight = work.tile(half_shape, F32, tag="straight", bufs=PRODUCT_BUFS)
            nc.vector.tensor_tensor(
                out=straight[:], in0=rope[:, :, :, here], in1=cos_bc[:, :, :, here], op=ALU.mult
            )
            crossed = work.tile(half_shape, F32, tag="crossed", bufs=PRODUCT_BUFS)
            nc.vector.tensor_tensor(
                out=crossed[:], in0=rope[:, :, :, there], in1=sin_bc[:, :, :, here], op=ALU.mult
            )
            nc.gpsimd.tensor_tensor(out=rot_of[n][:, :, :, here], in0=straight[:], in1=crossed[:], op=sum_op)

        def rotate_low(n):
            rot_of[n] = results.tile([P, UNIT_TILES, HEADS, ROPE], F32, name="rot_sb", tag="rot")
            rotate(n, LOW, HIGH, ALU.subtract)

        def rotate_high(n):
            rotate(n, HIGH, LOW, ALU.add)
            tiles = slice(n * UNIT_TILES, (n + 1) * UNIT_TILES)
            nc.sync.dma_start(out=rot_dram[:, tiles, :], in_=rot_of[n][:].rearrange("p t h d -> p t (h d)"))

        wa_scaled = scale_weight(nc.vector, "wa", wa_raw, sa_bc)
        for m in range(WEIGHT_HALVES):
            transpose_weight(wa_grouped, wa_scaled, "p (o c d) u -> p o c d u", m)
            quantise_weight(wa_grouped, wa_codes, wa_scales, slice(m * UNIT_TILES * P, (m + 1) * UNIT_TILES * P))
            transpose_unit(0, m, x_loads[m][:])
            group_unit(0, m)
        wb_scaled = scale_weight(nc.gpsimd, "wb", wb_raw, sb_bc)

        def active(n):
            return 0 <= n < UNITS

        for i in range(UNITS + ROTATE_LAG):
            if active(i - ROTATE_LAG):
                rotate_low(i - ROTATE_LAG)
            if active(i):
                quantise_unit(0, i)
            if active(i - Q_LAG):
                quantise_unit(1, i - Q_LAG)
            if active(i - 1):
                invert(i - 1)
            if active(i - ROTATE_LAG):
                rotate_high(i - ROTATE_LAG)
            if active(i - 1):
                normalise(i - 1)
            if active(i):
                first_matmul(i)
            if active(i - Q_LAG):
                second_matmul_rotated(i - Q_LAG)
                second_matmul_plain(i - Q_LAG)
            if active(i + X_LEAD):
                transpose_unit(0, i + X_LEAD, x_loads[i + X_LEAD][:])
            if active(i - 1):
                transpose_unit(1, i - 1, h_of[i - 1][:])
            if active(i):
                sum_squares(i)
            if active(i - Q_LAG):
                store_plain(i - Q_LAG)
            if active(i):
                root(i)
            if active(i + X_LEAD):
                group_unit(0, i + X_LEAD)
            if active(i - 1):
                group_unit(1, i - 1)
            if i == WB_TRANSPOSE_ROUND:
                for m in range(WEIGHT_HALVES):
                    transpose_weight(wb_grouped, wb_scaled, "p (c o d) u -> p o c d u", m)
            if i == WB_QUANTISE_ROUND:
                quantise_weight(wb_grouped, wb_codes, wb_scales, slice(0, OUT))
